import numpy as np
import ml_dtypes


def mxq(x, axis, fmt="e4m3"):
    dtype, down = {"e4m3": (ml_dtypes.float8_e4m3fn, 7), "e5m2": (ml_dtypes.float8_e5m2, 14)}[fmt]
    v = np.moveaxis(np.asarray(x, np.float32).astype(ml_dtypes.bfloat16).astype(np.float64), axis, -1)
    blocks = v.reshape(v.shape[:-1] + (-1, 32))
    amax = np.abs(blocks).max(-1, keepdims=True)
    byte = np.maximum(np.where(amax > 0, np.frexp(amax)[1] - 1 + 127, 0) - down, 1)
    scale = np.exp2(byte - 127.0)
    codes = (blocks / scale).astype(np.float32).astype(dtype).astype(np.float64)
    return np.moveaxis((codes * scale).reshape(v.shape), -1, axis)


WIDE = False


def mx_kscale(k):
    if not WIDE:
        return np.ones(k)
    levels = np.array([10, -10, 5, -5, 0])
    a = np.random.permutation(np.resize(levels, k // 512 * 4)).reshape(k // 512, 4)
    idx = np.arange(k)
    return np.exp2(a[idx // 512, idx % 128 // 32])


BF16 = ml_dtypes.bfloat16


def bf(x):
    return np.asarray(x, np.float32).astype(BF16)


def f64(x):
    return np.asarray(x).astype(np.float64)


B, D_IN, H, D_OUT = 512, 4096, 2048, 1024
H2 = 2 * H
LN_EPS = 1e-5


def setup_inputs():
    s = mx_kscale(H)
    t = mx_kscale(H2)
    return {
        "h1": bf(np.tanh(np.random.standard_normal((B, H))) * s),
        "W_ih1": bf(np.random.standard_normal((H, H)) / np.sqrt(H) / s[None, :]),
        "b_ih1": bf(0.25 + 0.3 * np.random.standard_normal(H)),
        "b_hh1": bf(0.3 * np.random.standard_normal(H)),
        "ln_g": bf((1.0 + 0.1 * np.random.standard_normal(H2)) * t),
        "ln_b": bf(0.2 * np.random.standard_normal(H2) * t),
        "fc_W": bf(np.random.standard_normal((D_OUT, H2)) / np.sqrt(H2) / t[None, :]),
        "fc_b": bf(0.3 * np.random.standard_normal(D_OUT)),
    }


def reference(h1, W_ih1, b_ih1, b_hh1, ln_g, ln_b, fc_W, fc_b):
    h2 = np.tanh((mxq(f64(h1), 1, "e4m3") @ mxq(f64(W_ih1), 1, "e4m3").T) + f64(b_ih1) + f64(b_hh1))
    combined = np.concatenate([h2, h2], axis=1)
    mu = combined.mean(axis=-1, keepdims=True)
    var = combined.var(axis=-1, keepdims=True)
    normed = (combined - mu) / np.sqrt(var + LN_EPS) * f64(ln_g) + f64(ln_b)
    return (mxq(normed, 1, "e4m3") @ mxq(f64(fc_W), 1, "e4m3").T) + f64(fc_b)

@@ -1,0 +1,275 @@
+from contextlib import ExitStack
+
+import concourse.mybir as mybir
+from concourse.masks import make_identity
+
+F32 = mybir.dt.float32
+BF16 = mybir.dt.bfloat16
+U32 = mybir.dt.uint32
+U8 = mybir.dt.uint8
+FP8X4 = mybir.dt.float8_e4m3fn_x4
+ALU = mybir.AluOpType
+ACT = mybir.ActivationFunctionType
+
+P = 128
+B, H, D_OUT = 512, 2048, 1024
+LN_EPS = 1e-5
+FLOPS = 2 * B * H * H + 2 * B * 2 * H * D_OUT
+
+
+def tile_rnnclassifier_pa_kernel(tc, h1, W_ih1, b_ih1, b_hh1, ln_g, ln_b, fc_W, fc_b, out):
+    nc = tc.nc
+    with ExitStack() as ctx:
+        const = ctx.enter_context(tc.tile_pool(name="const", bufs=1))
+        rawp = ctx.enter_context(tc.tile_pool(name="raw", bufs=4))
+        grpp = ctx.enter_context(tc.tile_pool(name="grouped", bufs=3))
+        wcp = ctx.enter_context(tc.tile_pool(name="wcodes", bufs=3))
+        plp = ctx.enter_context(tc.tile_pool(name="planes", bufs=4))
+        gnp = ctx.enter_context(tc.tile_pool(name="gnorm", bufs=2))
+        osp = ctx.enter_context(tc.tile_pool(name="outs", bufs=4))
+        tps = ctx.enter_context(tc.psum_pool(name="tps", bufs=4))
+        accp = ctx.enter_context(tc.psum_pool(name="accp", bufs=4))
+
+        def slab_src(k):
+            if k < 2:
+                return h1[k * 256:(k + 1) * 256, :].rearrange("(t p) k -> p t k", p=P), 2
+            if k < 10:
+                s = k - 2
+                return W_ih1[s * 256:(s + 1) * 256, :].rearrange("(q e) k -> q (e k)", e=2), 1
+            f = k - 10
+            cc, kq = f // 4, f % 4
+            return fc_W[cc * 512:(cc + 1) * 512, kq * 1024:(kq + 1) * 1024].rearrange("(c p) k -> p c k", p=P), 4
+
+        def slab_off(k, i, a, u):
+            if k < 2:
+                return (i // 2) * 1024 + (2 * (i % 2) + a) * 256 + u * 128
+            if k < 10:
+                return a * 1024 + i * 256 + u * 128
+            return (2 * (i % 2) + a) * 512 + (i // 2) * 256 + u * 128
+
+        raws = {}
+        groupeds = {}
+        codes = {}
+        scales = {}
+
+        def load(k):
+            raw = rawp.tile([P, 4096], BF16, name="raw", tag="raw")
+            src, parts = slab_src(k)
+            if parts == 1:
+                nc.sync.dma_start(out=raw[:], in_=src)
+            else:
+                nc.sync.dma_start(out=raw[:].rearrange("p (t k) -> p t k", t=parts), in_=src)
+            raws[k] = raw
+
+        def transpose_copy(k):
+            raw_w = raws[k][:].bitcast(F32)
+            grouped = grpp.tile([P, 4096], BF16, name="grouped", tag="grouped", align_bytes=64)
+            gw = grouped[:].bitcast(F32)
+            for i in range(4):
+                xt = tps.tile([P, 512], F32, name="xt", tag="tp")
+                for a in range(2):
+                    for u in range(2):
+                        o = slab_off(k, i, a, u)
+                        j = 2 * a + u
+                        nc.tensor.transpose(xt[:, j * 128:(j + 1) * 128], raw_w[:, o:o + 128], ident[:])
+                nc.scalar.copy(
+                    out=gw[:, i * 512:(i + 1) * 512].rearrange("p (a c u) -> p a c u", a=2, u=2),
+                    in_=xt[:].rearrange("p (a u c) -> p a c u", a=2, u=2),
+                )
+            groupeds[k] = grouped
+
+        def quantise(k):
+            if 2 <= k < 10:
+                cd = wcp.tile([P, 1024], U32, name="wc", tag="wc", align_bytes=64)
+                sc = wcp.tile([P, 1024], U8, name="ws", tag="ws", align_bytes=64)
+            else:
+                cd = const.tile([P, 1024], U32, name="cd%d" % k, align_bytes=64)
+                sc = const.tile([P, 1024], U8, name="sc%d" % k, align_bytes=64)
+            nc.vector.quantize_mx(out=cd[:].bitcast(FP8X4), scales=sc[:], in_=groupeds[k][:])
+            codes[k] = cd
+            scales[k] = sc
+
+        for k in range(4):
+            load(k)
+
+        ident = const.tile([P, P], F32, name="ident")
+        make_identity(nc, ident[:])
+        ones = const.tile([P, P], BF16, name="ones")
+        nc.vector.memset(ones[:], 1.0)
+        brow = const.tile([P, 3072], BF16, name="brow")
+        nc.vector.memset(brow[:], 0.0)
+        nc.scalar.dma_start(out=brow[0:1, 0:2048], in_=b_ih1.rearrange("(o n) -> o n", o=1))
+        nc.scalar.dma_start(out=brow[1:2, 0:2048], in_=b_hh1.rearrange("(o n) -> o n", o=1))
+        nc.scalar.dma_start(out=brow[0:1, 2048:3072], in_=fc_b.rearrange("(o n) -> o n", o=1))
+        gl = const.tile([P, 256], BF16, name="gl")
+        nc.vector.memset(gl[:], 0.0)
+        nc.scalar.dma_start(out=gl[0:16, :], in_=ln_g.rearrange("(r c) -> r c", c=256))
+        nc.scalar.dma_start(out=gl[16:32, :], in_=ln_b.rearrange("(r c) -> r c", c=256))
+        mhalf = const.tile([P, 4], F32, name="mhalf")
+        nc.vector.memset(mhalf[:], -0.5)
+
+        bias1 = const.tile([P, 2048], F32, name="bias1")
+        fcb = const.tile([P, 1024], F32, name="fcb")
+        for c in range(6):
+            bp = accp.tile([P, 512], F32, name="bp", tag="acc")
+            nc.tensor.matmul(out=bp[:], lhsT=ones[:], rhs=brow[:, c * 512:(c + 1) * 512], start=True, stop=True)
+            if c < 4:
+                nc.vector.tensor_copy(
+                    out=bias1[:, c * 512:(c + 1) * 512].rearrange("p (s e q) -> p s e q", s=2, e=2),
+                    in_=bp[:].rearrange("p (s q e) -> p s e q", s=2, e=2),
+                )
+            else:
+                nc.vector.tensor_copy(out=fcb[:, (c - 4) * 512:(c - 3) * 512], in_=bp[:])
+        gps = tps.tile([P, 512], F32, name="gps", tag="tp")
+        nc.tensor.transpose(gps[:, 0:128], gl[:].bitcast(F32), ident[:])
+        gb = const.tile([P, 64], F32, name="gb")
+        nc.vector.tensor_copy(out=gb[:], in_=gps[:, 0:32].bitcast(BF16))
+
+        h2 = const.tile([P, 4, 2048], F32, name="h2")
+        stats = const.tile([P, 4, 4, 6], F32, name="stats")
+        mv = const.tile([P, 4, 2], F32, name="mv")
+        veps = const.tile([P, 4], F32, name="veps")
+        rstd = const.tile([P, 4], F32, name="rstd")
+        ncod = const.tile([P, 8 * 512], U32, name="ncod", align_bytes=64)
+        nsca = const.tile([P, 8 * 512], U8, name="nsca", align_bytes=64)
+
+        def mm1(s):
+            wc, ws = codes[s + 2], scales[s + 2]
+            for x in range(2):
+                acc = accp.tile([P, 512], F32, name="acc1", tag="acc")
+                for b2 in range(2):
+                    for g in range(4):
+                        lc = slice((b2 * 4 + g) * 128, (b2 * 4 + g + 1) * 128)
+                        rc = slice(g * 256, (g + 1) * 256)
+                        nc.tensor.matmul_mx(
+                            out=acc[:, b2 * 256:(b2 + 1) * 256],
+                            lhsT=codes[x][:, lc].bitcast(FP8X4), lhsT_scale=scales[x][:, lc],
+                            rhs=wc[:, rc].bitcast(FP8X4), rhs_scale=ws[:, rc],
+                            start=(g == 0), stop=(g == 3),
+                        )
+                hv = h2[:, 2 * x:2 * x + 2, s * 256:(s + 1) * 256]
+                nc.vector.tensor_tensor(
+                    out=hv, in0=acc[:].rearrange("p (b n) -> p b n", b=2),
+                    in1=bias1[:, s * 256:(s + 1) * 256].unsqueeze(1).to_broadcast([P, 2, 256]), op=ALU.add,
+                )
+                nc.scalar.activation(out=hv, in_=hv, func=ACT.Tanh)
+            if s % 2 == 1:
+                g = s // 2
+                for bt in range(4):
+                    nc.vector.bn_stats(out=stats[:, bt, g, :], in_=h2[:, bt, g * 512:(g + 1) * 512])
+
+        transpose_copy(0)
+        load(4)
+        transpose_copy(1)
+        load(5)
+        quantise(0)
+        transpose_copy(2)
+        load(6)
+        quantise(1)
+        transpose_copy(3)
+        load(7)
+        quantise(2)
+        for s in range(8):
+            k = s + 2
+            mm1(s)
+            transpose_copy(k + 2)
+            load(k + 6)
+            quantise(k + 1)
+
+        for bt in range(4):
+            nc.vector.bn_aggr(out=mv[:, bt, :], in_=stats[:, bt, :, :].rearrange("p g s -> p (g s)"))
+        nc.vector.tensor_scalar(out=veps[:], in0=mv[:, :, 1], scalar1=LN_EPS, scalar2=None, op0=ALU.add)
+        nc.gpsimd.tensor_tensor(out=rstd[:], in0=veps[:], in1=mhalf[:], op=ALU.pow)
+
+        def zpass(g):
+            for bt in range(4):
+                hv = h2[:, bt, g * 512:(g + 1) * 512]
+                nc.vector.tensor_scalar(out=hv, in0=hv, scalar1=mv[:, bt, 0:1], scalar2=rstd[:, bt:bt + 1],
+                                        op0=ALU.subtract, op1=ALU.mult)
+
+        planes = {}
+
+        def zt_gb(g):
+            for h in range(2):
+                planes[(h, g)] = plp.tile([P, 4, 512], BF16, name="planes", tag="planes")
+            for t in range(4):
+                u, e = t // 2, t % 2
+                s = 2 * g + u
+                zt = tps.tile([P, 512], F32, name="zt", tag="tp")
+                for bt in range(4):
+                    c0 = s * 256 + e * 128
+                    nc.tensor.transpose(zt[:, bt * 128:(bt + 1) * 128], h2[:, bt, c0:c0 + 128], ident[:])
+                for h in range(2):
+                    col = 16 * h + 2 * s + e
+                    nc.scalar.activation(out=planes[(h, g)][:, t, :], in_=zt[:], func=ACT.Identity,
+                                         scale=gb[:, col:col + 1], bias=gb[:, 32 + col:33 + col])
+
+        def regroup_quantise(g):
+            gns = []
+            for h in range(2):
+                gn = gnp.tile([P, 512, 4], BF16, name="gn", tag="gn", align_bytes=64)
+                nc.vector.tensor_copy(
+                    out=gn[:].rearrange("p (c i) t -> p c t i", i=4),
+                    in_=planes[(h, g)][:].rearrange("p t (c i) -> p c t i", i=4),
+                )
+                gns.append(gn)
+            for h in range(2):
+                kp = 4 * h + g
+                nc.vector.quantize_mx(out=ncod[:, kp * 512:(kp + 1) * 512].bitcast(FP8X4),
+                                      scales=nsca[:, kp * 512:(kp + 1) * 512],
+                                      in_=gns[h][:].rearrange("p b t -> p (b t)"))
+
+        acc2 = {}
+
+        def mm2(cc, kp, first, last):
+            f = 10 + cc * 4 + kp // 2
+            rc = slice((kp % 2) * 512, (kp % 2 + 1) * 512)
+            for bt in range(4):
+                if first:
+                    acc2[bt] = accp.tile([P, 512], F32, name="acc2", tag="acc")
+                lc = slice(kp * 512 + bt * 128, kp * 512 + (bt + 1) * 128)
+                nc.tensor.matmul_mx(
+                    out=acc2[bt][:],
+                    lhsT=ncod[:, lc].bitcast(FP8X4), lhsT_scale=nsca[:, lc],
+                    rhs=codes[f][:, rc].bitcast(FP8X4), rhs_scale=scales[f][:, rc],
+                    start=first, stop=last,
+                )
+
+        def store(cc):
+            for bt in range(4):
+                osb = osp.tile([P, 512], F32, name="osb", tag="osb")
+                nc.vector.tensor_tensor(out=osb[:], in0=acc2[bt][:], in1=fcb[:, cc * 512:(cc + 1) * 512], op=ALU.add)
+                nc.sync.dma_start(out=out[bt * 128:(bt + 1) * 128, cc * 512:(cc + 1) * 512], in_=osb[:])
+
+        zpass(0)
+        zt_gb(0)
+        zpass(1)
+        transpose_copy(12)
+        load(16)
+        quantise(11)
+        transpose_copy(13)
+        load(17)
+        quantise(12)
+        quantise(13)
+        for g in range(4):
+            regroup_quantise(g)
+            if g < 3:
+                zt_gb(g + 1)
+            if g < 2:
+                zpass(g + 2)
+            mm2(0, g, g == 0, False)
+            mm2(0, 4 + g, False, g == 3)
+        transpose_copy(14)
+        transpose_copy(15)
+        quantise(14)
+        store(0)
+        transpose_copy(16)
+        quantise(15)
+        for kq in range(4):
+            if kq < 1:
+                transpose_copy(17)
+            if kq < 2:
+                quantise(16 + kq)
+            mm2(1, 2 * kq, kq == 0, False)
+            mm2(1, 2 * kq + 1, False, kq == 3)
+        store(1)

@@ -29,16 +29,7 @@ def tile_rnnclassifier_pa_kernel(tc, h1, W_ih1, b_ih1, b_hh1, ln_g, ln_b, fc_W, 
         osp = ctx.enter_context(tc.tile_pool(name="outs", bufs=4))
         tps = ctx.enter_context(tc.psum_pool(name="tps", bufs=4))
         accp = ctx.enter_context(tc.psum_pool(name="accp", bufs=4))
-
-        def slab_src(k):
-            if k < 2:
-                return h1[k * 256:(k + 1) * 256, :].rearrange("(t p) k -> p t k", p=P), 2
-            if k < 10:
-                s = k - 2
-                return W_ih1[s * 256:(s + 1) * 256, :].rearrange("(q e) k -> q (e k)", e=2), 1
-            f = k - 10
-            cc, kq = f // 4, f % 4
-            return fc_W[cc * 512:(cc + 1) * 512, kq * 1024:(kq + 1) * 1024].rearrange("(c p) k -> p c k", p=P), 4
+        ctx.enter_context(tc.manual_schedule())
 
         def slab_off(k, i, a, u):
             if k < 2:
@@ -48,23 +39,42 @@ def tile_rnnclassifier_pa_kernel(tc, h1, W_ih1, b_ih1, b_hh1, ln_g, ln_b, fc_W, 
             return (2 * (i % 2) + a) * 512 + (i // 2) * 256 + u * 128
 
         raws = {}
+        banks = {}
         groupeds = {}
         codes = {}
         scales = {}
+        order = [0, 2, 1] + list(range(3, 18))
+        loaded = []
 
-        def load(k):
+        def load():
+            if len(loaded) == len(order):
+                return
+            k = order[len(loaded)]
+            loaded.append(k)
             raw = rawp.tile([P, 4096], BF16, name="raw", tag="raw")
-            src, parts = slab_src(k)
-            if parts == 1:
-                nc.sync.dma_start(out=raw[:], in_=src)
-            else:
-                nc.sync.dma_start(out=raw[:].rearrange("p (t k) -> p t k", t=parts), in_=src)
             raws[k] = raw
+            if k == 0:
+                for i in range(4):
+                    nc.sync.dma_start(
+                        out=raw[:, i * 1024:(i + 1) * 1024],
+                        in_=h1[(i // 2) * 128:(i // 2 + 1) * 128, (i % 2) * 1024:(i % 2 + 1) * 1024],
+                    )
+            elif k == 1:
+                nc.sync.dma_start(out=raw[:].rearrange("p (t k) -> p t k", t=2),
+                                  in_=h1[256:512, :].rearrange("(t p) k -> p t k", p=P))
+            elif k < 10:
+                s = k - 2
+                nc.sync.dma_start(out=raw[:], in_=W_ih1[s * 256:(s + 1) * 256, :].rearrange("(q e) k -> q (e k)", e=2))
+            else:
+                cc, kq = (k - 10) // 4, (k - 10) % 4
+                nc.sync.dma_start(
+                    out=raw[:].rearrange("p (c k) -> p c k", c=4),
+                    in_=fc_W[cc * 512:(cc + 1) * 512, kq * 1024:(kq + 1) * 1024].rearrange("(c p) k -> p c k", p=P),
+                )
 
-        def transpose_copy(k):
+        def T(k):
             raw_w = raws[k][:].bitcast(F32)
-            grouped = grpp.tile([P, 4096], BF16, name="grouped", tag="grouped", align_bytes=64)
-            gw = grouped[:].bitcast(F32)
+            banks[k] = []
             for i in range(4):
                 xt = tps.tile([P, 512], F32, name="xt", tag="tp")
                 for a in range(2):
@@ -72,13 +82,21 @@ def tile_rnnclassifier_pa_kernel(tc, h1, W_ih1, b_ih1, b_hh1, ln_g, ln_b, fc_W, 
                         o = slab_off(k, i, a, u)
                         j = 2 * a + u
                         nc.tensor.transpose(xt[:, j * 128:(j + 1) * 128], raw_w[:, o:o + 128], ident[:])
-                nc.scalar.copy(
-                    out=gw[:, i * 512:(i + 1) * 512].rearrange("p (a c u) -> p a c u", a=2, u=2),
-                    in_=xt[:].rearrange("p (a u c) -> p a c u", a=2, u=2),
-                )
+                banks[k].append(xt)
+
+        def C(k, engines="SSSS"):
+            grouped = grpp.tile([P, 4096], BF16, name="grouped", tag="grouped", align_bytes=64)
+            gw = grouped[:].bitcast(F32)
+            for i in range(4):
+                dst = gw[:, i * 512:(i + 1) * 512].rearrange("p (a c u) -> p a c u", a=2, u=2)
+                src = banks[k][i][:].rearrange("p (a u c) -> p a c u", a=2, u=2)
+                if engines[i] == "S":
+                    nc.scalar.copy(out=dst, in_=src)
+                else:
+                    nc.vector.tensor_copy(out=dst, in_=src)
             groupeds[k] = grouped
 
-        def quantise(k):
+        def Q(k):
             if 2 <= k < 10:
                 cd = wcp.tile([P, 1024], U32, name="wc", tag="wc", align_bytes=64)
                 sc = wcp.tile([P, 1024], U8, name="ws", tag="ws", align_bytes=64)
@@ -89,8 +107,8 @@ def tile_rnnclassifier_pa_kernel(tc, h1, W_ih1, b_ih1, b_hh1, ln_g, ln_b, fc_W, 
             codes[k] = cd
             scales[k] = sc
 
-        for k in range(4):
-            load(k)
+        for i in range(4):
+            load()
 
         ident = const.tile([P, P], F32, name="ident")
         make_identity(nc, ident[:])
@@ -98,19 +116,21 @@ def tile_rnnclassifier_pa_kernel(tc, h1, W_ih1, b_ih1, b_hh1, ln_g, ln_b, fc_W, 
         nc.vector.memset(ones[:], 1.0)
         brow = const.tile([P, 3072], BF16, name="brow")
         nc.vector.memset(brow[:], 0.0)
+        gl = const.tile([P, 256], BF16, name="gl")
+        nc.vector.memset(gl[:], 0.0)
+        mhalf = const.tile([P, 4], F32, name="mhalf")
+        nc.vector.memset(mhalf[:], -0.5)
         nc.scalar.dma_start(out=brow[0:1, 0:2048], in_=b_ih1.rearrange("(o n) -> o n", o=1))
         nc.scalar.dma_start(out=brow[1:2, 0:2048], in_=b_hh1.rearrange("(o n) -> o n", o=1))
         nc.scalar.dma_start(out=brow[0:1, 2048:3072], in_=fc_b.rearrange("(o n) -> o n", o=1))
-        gl = const.tile([P, 256], BF16, name="gl")
-        nc.vector.memset(gl[:], 0.0)
         nc.scalar.dma_start(out=gl[0:16, :], in_=ln_g.rearrange("(r c) -> r c", c=256))
         nc.scalar.dma_start(out=gl[16:32, :], in_=ln_b.rearrange("(r c) -> r c", c=256))
-        mhalf = const.tile([P, 4], F32, name="mhalf")
-        nc.vector.memset(mhalf[:], -0.5)
 
         bias1 = const.tile([P, 2048], F32, name="bias1")
         fcb = const.tile([P, 1024], F32, name="fcb")
-        for c in range(6):
+        gb = const.tile([P, 64], F32, name="gb")
+
+        def BM(c):
             bp = accp.tile([P, 512], F32, name="bp", tag="acc")
             nc.tensor.matmul(out=bp[:], lhsT=ones[:], rhs=brow[:, c * 512:(c + 1) * 512], start=True, stop=True)
             if c < 4:
@@ -120,10 +140,11 @@ def tile_rnnclassifier_pa_kernel(tc, h1, W_ih1, b_ih1, b_hh1, ln_g, ln_b, fc_W, 
                 )
             else:
                 nc.vector.tensor_copy(out=fcb[:, (c - 4) * 512:(c - 3) * 512], in_=bp[:])
-        gps = tps.tile([P, 512], F32, name="gps", tag="tp")
-        nc.tensor.transpose(gps[:, 0:128], gl[:].bitcast(F32), ident[:])
-        gb = const.tile([P, 64], F32, name="gb")
-        nc.vector.tensor_copy(out=gb[:], in_=gps[:, 0:32].bitcast(BF16))
+
+        def GT():
+            gps = tps.tile([P, 512], F32, name="gps", tag="tp")
+            nc.tensor.transpose(gps[:, 0:128], gl[:].bitcast(F32), ident[:])
+            nc.vector.tensor_copy(out=gb[:], in_=gps[:, 0:32].bitcast(BF16))
 
         h2 = const.tile([P, 4, 2048], F32, name="h2")
         stats = const.tile([P, 4, 4, 6], F32, name="stats")
@@ -132,144 +153,207 @@ def tile_rnnclassifier_pa_kernel(tc, h1, W_ih1, b_ih1, b_hh1, ln_g, ln_b, fc_W, 
         rstd = const.tile([P, 4], F32, name="rstd")
         ncod = const.tile([P, 8 * 512], U32, name="ncod", align_bytes=64)
         nsca = const.tile([P, 8 * 512], U8, name="nsca", align_bytes=64)
+        acc1 = {}
 
-        def mm1(s):
+        def MM1(s, x):
             wc, ws = codes[s + 2], scales[s + 2]
-            for x in range(2):
-                acc = accp.tile([P, 512], F32, name="acc1", tag="acc")
-                for b2 in range(2):
-                    for g in range(4):
-                        lc = slice((b2 * 4 + g) * 128, (b2 * 4 + g + 1) * 128)
-                        rc = slice(g * 256, (g + 1) * 256)
-                        nc.tensor.matmul_mx(
-                            out=acc[:, b2 * 256:(b2 + 1) * 256],
-                            lhsT=codes[x][:, lc].bitcast(FP8X4), lhsT_scale=scales[x][:, lc],
-                            rhs=wc[:, rc].bitcast(FP8X4), rhs_scale=ws[:, rc],
-                            start=(g == 0), stop=(g == 3),
-                        )
-                hv = h2[:, 2 * x:2 * x + 2, s * 256:(s + 1) * 256]
-                nc.vector.tensor_tensor(
-                    out=hv, in0=acc[:].rearrange("p (b n) -> p b n", b=2),
-                    in1=bias1[:, s * 256:(s + 1) * 256].unsqueeze(1).to_broadcast([P, 2, 256]), op=ALU.add,
-                )
-                nc.scalar.activation(out=hv, in_=hv, func=ACT.Tanh)
-            if s % 2 == 1:
-                g = s // 2
-                for bt in range(4):
-                    nc.vector.bn_stats(out=stats[:, bt, g, :], in_=h2[:, bt, g * 512:(g + 1) * 512])
+            acc = accp.tile([P, 512], F32, name="acc1", tag="acc")
+            acc1[(s, x)] = acc
+            for b2 in range(2):
+                for g in range(4):
+                    lc = slice((b2 * 4 + g) * 128, (b2 * 4 + g + 1) * 128)
+                    rc = slice(g * 256, (g + 1) * 256)
+                    nc.tensor.matmul_mx(
+                        out=acc[:, b2 * 256:(b2 + 1) * 256],
+                        lhsT=codes[x][:, lc].bitcast(FP8X4), lhsT_scale=scales[x][:, lc],
+                        rhs=wc[:, rc].bitcast(FP8X4), rhs_scale=ws[:, rc],
+                        start=(g == 0), stop=(g == 3),
+                    )
 
-        transpose_copy(0)
-        load(4)
-        transpose_copy(1)
-        load(5)
-        quantise(0)
-        transpose_copy(2)
-        load(6)
-        quantise(1)
-        transpose_copy(3)
-        load(7)
-        quantise(2)
-        for s in range(8):
-            k = s + 2
-            mm1(s)
-            transpose_copy(k + 2)
-            load(k + 6)
-            quantise(k + 1)
+        def BIAS(s, x):
+            nc.vector.tensor_tensor(
+                out=h2[:, 2 * x:2 * x + 2, s * 256:(s + 1) * 256],
+                in0=acc1[(s, x)][:].rearrange("p (b n) -> p b n", b=2),
+                in1=bias1[:, s * 256:(s + 1) * 256].unsqueeze(1).to_broadcast([P, 2, 256]), op=ALU.add,
+            )
 
-        for bt in range(4):
-            nc.vector.bn_aggr(out=mv[:, bt, :], in_=stats[:, bt, :, :].rearrange("p g s -> p (g s)"))
-        nc.vector.tensor_scalar(out=veps[:], in0=mv[:, :, 1], scalar1=LN_EPS, scalar2=None, op0=ALU.add)
-        nc.gpsimd.tensor_tensor(out=rstd[:], in0=veps[:], in1=mhalf[:], op=ALU.pow)
+        def TANH(s, x):
+            hv = h2[:, 2 * x:2 * x + 2, s * 256:(s + 1) * 256]
+            nc.scalar.activation(out=hv, in_=hv, func=ACT.Tanh)
 
-        def zpass(g):
+        def BN(bt, g):
+            nc.vector.bn_stats(out=stats[:, bt, g, :], in_=h2[:, bt, g * 512:(g + 1) * 512])
+
+        def STATS():
+            for bt in range(4):
+                nc.vector.bn_aggr(out=mv[:, bt, :], in_=stats[:, bt, :, :].rearrange("p g s -> p (g s)"))
+            nc.vector.tensor_scalar(out=veps[:], in0=mv[:, :, 1], scalar1=LN_EPS, scalar2=None, op0=ALU.add)
+            nc.gpsimd.tensor_tensor(out=rstd[:], in0=veps[:], in1=mhalf[:], op=ALU.pow)
+
+        def Z(g):
             for bt in range(4):
                 hv = h2[:, bt, g * 512:(g + 1) * 512]
                 nc.vector.tensor_scalar(out=hv, in0=hv, scalar1=mv[:, bt, 0:1], scalar2=rstd[:, bt:bt + 1],
                                         op0=ALU.subtract, op1=ALU.mult)
 
         planes = {}
+        zts = {}
+        gns = {}
 
-        def zt_gb(g):
+        def ZT(g):
             for h in range(2):
                 planes[(h, g)] = plp.tile([P, 4, 512], BF16, name="planes", tag="planes")
             for t in range(4):
-                u, e = t // 2, t % 2
-                s = 2 * g + u
+                c0 = (2 * g + t // 2) * 256 + (t % 2) * 128
                 zt = tps.tile([P, 512], F32, name="zt", tag="tp")
                 for bt in range(4):
-                    c0 = s * 256 + e * 128
                     nc.tensor.transpose(zt[:, bt * 128:(bt + 1) * 128], h2[:, bt, c0:c0 + 128], ident[:])
-                for h in range(2):
-                    col = 16 * h + 2 * s + e
-                    nc.scalar.activation(out=planes[(h, g)][:, t, :], in_=zt[:], func=ACT.Identity,
+                zts[(g, t)] = zt
+
+        def GB(g):
+            for h in range(2):
+                for t in range(4):
+                    col = 16 * h + 4 * g + t
+                    nc.scalar.activation(out=planes[(h, g)][:, t, :], in_=zts[(g, t)][:], func=ACT.Identity,
                                          scale=gb[:, col:col + 1], bias=gb[:, 32 + col:33 + col])
 
-        def regroup_quantise(g):
-            gns = []
-            for h in range(2):
-                gn = gnp.tile([P, 512, 4], BF16, name="gn", tag="gn", align_bytes=64)
-                nc.vector.tensor_copy(
-                    out=gn[:].rearrange("p (c i) t -> p c t i", i=4),
-                    in_=planes[(h, g)][:].rearrange("p t (c i) -> p c t i", i=4),
-                )
-                gns.append(gn)
-            for h in range(2):
-                kp = 4 * h + g
-                nc.vector.quantize_mx(out=ncod[:, kp * 512:(kp + 1) * 512].bitcast(FP8X4),
-                                      scales=nsca[:, kp * 512:(kp + 1) * 512],
-                                      in_=gns[h][:].rearrange("p b t -> p (b t)"))
+        def RG(g, h):
+            gn = gnp.tile([P, 512, 4], BF16, name="gn", tag="gn", align_bytes=64)
+            nc.vector.tensor_copy(
+                out=gn[:].rearrange("p (c i) t -> p c t i", i=4),
+                in_=planes[(h, g)][:].rearrange("p t (c i) -> p c t i", i=4),
+            )
+            gns[(h, g)] = gn
+
+        def QN(g, h):
+            kp = 4 * h + g
+            nc.vector.quantize_mx(out=ncod[:, kp * 512:(kp + 1) * 512].bitcast(FP8X4),
+                                  scales=nsca[:, kp * 512:(kp + 1) * 512],
+                                  in_=gns[(h, g)][:].rearrange("p b t -> p (b t)"))
 
         acc2 = {}
 
-        def mm2(cc, kp, first, last):
+        def MM2(cc, kp, bt, first, last):
             f = 10 + cc * 4 + kp // 2
             rc = slice((kp % 2) * 512, (kp % 2 + 1) * 512)
-            for bt in range(4):
-                if first:
-                    acc2[bt] = accp.tile([P, 512], F32, name="acc2", tag="acc")
-                lc = slice(kp * 512 + bt * 128, kp * 512 + (bt + 1) * 128)
-                nc.tensor.matmul_mx(
-                    out=acc2[bt][:],
-                    lhsT=ncod[:, lc].bitcast(FP8X4), lhsT_scale=nsca[:, lc],
-                    rhs=codes[f][:, rc].bitcast(FP8X4), rhs_scale=scales[f][:, rc],
-                    start=first, stop=last,
-                )
+            if first:
+                acc2[bt] = accp.tile([P, 512], F32, name="acc2", tag="acc")
+            lc = slice(kp * 512 + bt * 128, kp * 512 + (bt + 1) * 128)
+            nc.tensor.matmul_mx(
+                out=acc2[bt][:],
+                lhsT=ncod[:, lc].bitcast(FP8X4), lhsT_scale=nsca[:, lc],
+                rhs=codes[f][:, rc].bitcast(FP8X4), rhs_scale=scales[f][:, rc],
+                start=first, stop=last,
+            )
 
-        def store(cc):
+        def MM2all(cc, kp, first, last):
             for bt in range(4):
-                osb = osp.tile([P, 512], F32, name="osb", tag="osb")
-                nc.vector.tensor_tensor(out=osb[:], in0=acc2[bt][:], in1=fcb[:, cc * 512:(cc + 1) * 512], op=ALU.add)
-                nc.sync.dma_start(out=out[bt * 128:(bt + 1) * 128, cc * 512:(cc + 1) * 512], in_=osb[:])
+                MM2(cc, kp, bt, first, last)
 
-        zpass(0)
-        zt_gb(0)
-        zpass(1)
-        transpose_copy(12)
-        load(16)
-        quantise(11)
-        transpose_copy(13)
-        load(17)
-        quantise(12)
-        quantise(13)
+        def OUT(cc, bt):
+            osb = osp.tile([P, 512], F32, name="osb", tag="osb")
+            nc.vector.tensor_tensor(out=osb[:], in0=acc2[bt][:], in1=fcb[:, cc * 512:(cc + 1) * 512], op=ALU.add)
+            nc.sync.dma_start(out=out[bt * 128:(bt + 1) * 128, cc * 512:(cc + 1) * 512], in_=osb[:])
+
+        T(0)
+        C(0)
+        load()
+        for c in range(4):
+            BM(c)
+        T(2)
+        C(2)
+        load()
+        Q(0)
+        BM(4)
+        BM(5)
+        GT()
+        T(1)
+        C(1)
+        load()
+        Q(2)
+        MM1(0, 0)
+        T(3)
+        C(3)
+        load()
+        Q(1)
+        BIAS(0, 0)
+        MM1(0, 1)
+        T(4)
+        T(5)
+        load()
+        load()
+        C(4)
+        Q(3)
+        BIAS(0, 1)
+        for s in range(1, 8):
+            k = s + 2
+            MM1(s, 0)
+            MM1(s, 1)
+            T(k + 3)
+            load()
+            TANH(s - 1, 0)
+            TANH(s - 1, 1)
+            C(k + 2)
+            Q(k + 1)
+            if s % 2 == 0:
+                BN(0, s // 2 - 1)
+                BN(1, s // 2 - 1)
+            elif s > 1:
+                BN(2, s // 2 - 1)
+                BN(3, s // 2 - 1)
+            BIAS(s, 0)
+            BIAS(s, 1)
+        for i in range(4):
+            load()
+        TANH(7, 0)
+        TANH(7, 1)
+        C(12)
+        T(13)
+        C(13)
+        for bt in range(4):
+            BN(bt, 3)
+        STATS()
+        Q(11)
+        Q(12)
+        Z(0)
+        ZT(0)
+        GB(0)
+        Z(1)
+        Q(13)
         for g in range(4):
-            regroup_quantise(g)
             if g < 3:
-                zt_gb(g + 1)
+                ZT(g + 1)
+            RG(g, 0)
+            if g < 3:
+                GB(g + 1)
+            RG(g, 1)
+            QN(g, 0)
+            QN(g, 1)
             if g < 2:
-                zpass(g + 2)
-            mm2(0, g, g == 0, False)
-            mm2(0, 4 + g, False, g == 3)
-        transpose_copy(14)
-        transpose_copy(15)
-        quantise(14)
-        store(0)
-        transpose_copy(16)
-        quantise(15)
-        for kq in range(4):
-            if kq < 1:
-                transpose_copy(17)
-            if kq < 2:
-                quantise(16 + kq)
-            mm2(1, 2 * kq, kq == 0, False)
-            mm2(1, 2 * kq + 1, False, kq == 3)
-        store(1)
+                Z(g + 2)
+            MM2all(0, g, g == 0, False)
+            MM2all(0, 4 + g, False, g == 3)
+        T(14)
+        C(14, "SSSV")
+        T(15)
+        C(15, "SSSV")
+        Q(14)
+        for bt in range(4):
+            OUT(0, bt)
+        T(16)
+        C(16, "SSSV")
+        Q(15)
+        MM2all(1, 0, True, False)
+        MM2all(1, 1, False, False)
+        T(17)
+        C(17, "SSSV")
+        Q(16)
+        MM2all(1, 2, False, False)
+        MM2all(1, 3, False, False)
+        Q(17)
+        MM2all(1, 4, False, False)
+        MM2all(1, 5, False, False)
+        for bt in range(4):
+            MM2(1, 6, bt, False, False)
+            MM2(1, 7, bt, False, True)
+            OUT(1, bt)

@@ -17,95 +17,110 @@ LN_EPS = 1e-5
 FLOPS = 2 * B * H * H + 2 * B * 2 * H * D_OUT
 
 
+N0 = (10, 17)
+RG_LAG = (3, 4)
+MM_LAG = (4, 5)
+N_STEPS = 29
+
+
 def tile_rnnclassifier_pa_kernel(tc, h1, W_ih1, b_ih1, b_hh1, ln_g, ln_b, fc_W, fc_b, out):
     nc = tc.nc
     with ExitStack() as ctx:
         const = ctx.enter_context(tc.tile_pool(name="const", bufs=1))
         rawp = ctx.enter_context(tc.tile_pool(name="raw", bufs=4))
         grpp = ctx.enter_context(tc.tile_pool(name="grouped", bufs=3))
-        wcp = ctx.enter_context(tc.tile_pool(name="wcodes", bufs=3))
+        wfp = ctx.enter_context(tc.tile_pool(name="wfcodes", bufs=10))
         plp = ctx.enter_context(tc.tile_pool(name="planes", bufs=4))
-        gnp = ctx.enter_context(tc.tile_pool(name="gnorm", bufs=2))
+        gnp = ctx.enter_context(tc.tile_pool(name="gnorm", bufs=3))
         osp = ctx.enter_context(tc.tile_pool(name="outs", bufs=4))
-        tps = ctx.enter_context(tc.psum_pool(name="tps", bufs=4))
-        accp = ctx.enter_context(tc.psum_pool(name="accp", bufs=4))
+        psp = ctx.enter_context(tc.psum_pool(name="psum", bufs=8))
         ctx.enter_context(tc.manual_schedule())
 
-        def slab_off(k, i, a, u):
-            if k < 2:
+        def bank(name):
+            return psp.tile([P, 512], F32, name=name, tag="ps")
+
+        def slab_off(pos, i, a, u):
+            if pos == 0 or pos == 9:
                 return (i // 2) * 1024 + (2 * (i % 2) + a) * 256 + u * 128
-            if k < 10:
+            if pos < 9:
                 return a * 1024 + i * 256 + u * 128
-            return (2 * (i % 2) + a) * 512 + (i // 2) * 256 + u * 128
+            return (2 * i + a) * 256 + u * 128
 
         raws = {}
         banks = {}
         groupeds = {}
         codes = {}
         scales = {}
-        order = [0, 2, 1] + list(range(3, 18))
         loaded = []
 
         def load():
-            if len(loaded) == len(order):
+            pos = len(loaded)
+            if pos >= 18:
                 return
-            k = order[len(loaded)]
-            loaded.append(k)
+            loaded.append(pos)
             raw = rawp.tile([P, 4096], BF16, name="raw", tag="raw")
-            raws[k] = raw
-            if k == 0:
+            raws[pos] = raw
+            if pos == 0:
                 for i in range(4):
                     nc.sync.dma_start(
                         out=raw[:, i * 1024:(i + 1) * 1024],
                         in_=h1[(i // 2) * 128:(i // 2 + 1) * 128, (i % 2) * 1024:(i % 2 + 1) * 1024],
                     )
-            elif k == 1:
+            elif pos == 9:
                 nc.sync.dma_start(out=raw[:].rearrange("p (t k) -> p t k", t=2),
                                   in_=h1[256:512, :].rearrange("(t p) k -> p t k", p=P))
-            elif k < 10:
-                s = k - 2
+            elif pos < 9:
+                s = pos - 1
                 nc.sync.dma_start(out=raw[:], in_=W_ih1[s * 256:(s + 1) * 256, :].rearrange("(q e) k -> q (e k)", e=2))
             else:
-                cc, kq = (k - 10) // 4, (k - 10) % 4
+                f = pos - 10
+                kp = 4 * (f % 2) + f // 2
                 nc.sync.dma_start(
-                    out=raw[:].rearrange("p (c k) -> p c k", c=4),
-                    in_=fc_W[cc * 512:(cc + 1) * 512, kq * 1024:(kq + 1) * 1024].rearrange("(c p) k -> p c k", p=P),
+                    out=raw[:].rearrange("p (c k) -> p c k", c=8),
+                    in_=fc_W[:, kp * 512:(kp + 1) * 512].rearrange("(c p) k -> p c k", p=P),
                 )
 
-        def T(k):
-            raw_w = raws[k][:].bitcast(F32)
-            banks[k] = []
+        def T(pos):
+            if pos >= 18:
+                return
+            raw_w = raws[pos][:].bitcast(F32)
+            banks[pos] = []
             for i in range(4):
-                xt = tps.tile([P, 512], F32, name="xt", tag="tp")
+                xt = bank("xt")
                 for a in range(2):
                     for u in range(2):
-                        o = slab_off(k, i, a, u)
+                        o = slab_off(pos, i, a, u)
                         j = 2 * a + u
                         nc.tensor.transpose(xt[:, j * 128:(j + 1) * 128], raw_w[:, o:o + 128], ident[:])
-                banks[k].append(xt)
+                banks[pos].append(xt)
+            load()
 
-        def C(k, engines="SSSS"):
+        def C(pos, vector_share):
+            if pos >= 18:
+                return
             grouped = grpp.tile([P, 4096], BF16, name="grouped", tag="grouped", align_bytes=64)
             gw = grouped[:].bitcast(F32)
             for i in range(4):
                 dst = gw[:, i * 512:(i + 1) * 512].rearrange("p (a c u) -> p a c u", a=2, u=2)
-                src = banks[k][i][:].rearrange("p (a u c) -> p a c u", a=2, u=2)
-                if engines[i] == "S":
-                    nc.scalar.copy(out=dst, in_=src)
-                else:
+                src = banks[pos][i][:].rearrange("p (a u c) -> p a c u", a=2, u=2)
+                if i >= 4 - vector_share:
                     nc.vector.tensor_copy(out=dst, in_=src)
-            groupeds[k] = grouped
+                else:
+                    nc.scalar.copy(out=dst, in_=src)
+            groupeds[pos] = grouped
 
-        def Q(k):
-            if 2 <= k < 10:
-                cd = wcp.tile([P, 1024], U32, name="wc", tag="wc", align_bytes=64)
-                sc = wcp.tile([P, 1024], U8, name="ws", tag="ws", align_bytes=64)
+        def Q(pos):
+            if pos >= 18:
+                return
+            if pos == 0 or pos == 9:
+                cd = const.tile([P, 1024], U32, name="hcd%d" % pos, align_bytes=64)
+                sc = const.tile([P, 1024], U8, name="hsc%d" % pos, align_bytes=64)
             else:
-                cd = const.tile([P, 1024], U32, name="cd%d" % k, align_bytes=64)
-                sc = const.tile([P, 1024], U8, name="sc%d" % k, align_bytes=64)
-            nc.vector.quantize_mx(out=cd[:].bitcast(FP8X4), scales=sc[:], in_=groupeds[k][:])
-            codes[k] = cd
-            scales[k] = sc
+                cd = wfp.tile([P, 1024], U32, name="cd", tag="cd", align_bytes=64)
+                sc = wfp.tile([P, 1024], U8, name="sc", tag="sc", align_bytes=64)
+            nc.vector.quantize_mx(out=cd[:].bitcast(FP8X4), scales=sc[:], in_=groupeds[pos][:])
+            codes[pos] = cd
+            scales[pos] = sc
 
         for i in range(4):
             load()
@@ -131,7 +146,7 @@ def tile_rnnclassifier_pa_kernel(tc, h1, W_ih1, b_ih1, b_hh1, ln_g, ln_b, fc_W, 
         gb = const.tile([P, 64], F32, name="gb")
 
         def BM(c):
-            bp = accp.tile([P, 512], F32, name="bp", tag="acc")
+            bp = bank("bp")
             nc.tensor.matmul(out=bp[:], lhsT=ones[:], rhs=brow[:, c * 512:(c + 1) * 512], start=True, stop=True)
             if c < 4:
                 nc.vector.tensor_copy(
@@ -142,7 +157,7 @@ def tile_rnnclassifier_pa_kernel(tc, h1, W_ih1, b_ih1, b_hh1, ln_g, ln_b, fc_W, 
                 nc.vector.tensor_copy(out=fcb[:, (c - 4) * 512:(c - 3) * 512], in_=bp[:])
 
         def GT():
-            gps = tps.tile([P, 512], F32, name="gps", tag="tp")
+            gps = bank("gps")
             nc.tensor.transpose(gps[:, 0:128], gl[:].bitcast(F32), ident[:])
             nc.vector.tensor_copy(out=gb[:], in_=gps[:, 0:32].bitcast(BF16))
 
@@ -151,13 +166,14 @@ def tile_rnnclassifier_pa_kernel(tc, h1, W_ih1, b_ih1, b_hh1, ln_g, ln_b, fc_W, 
         mv = const.tile([P, 4, 2], F32, name="mv")
         veps = const.tile([P, 4], F32, name="veps")
         rstd = const.tile([P, 4], F32, name="rstd")
-        ncod = const.tile([P, 8 * 512], U32, name="ncod", align_bytes=64)
-        nsca = const.tile([P, 8 * 512], U8, name="nsca", align_bytes=64)
+        ncod = [const.tile([P, 8 * 256], U32, name="ncod%d" % x, align_bytes=64) for x in range(2)]
+        nsca = [const.tile([P, 8 * 256], U8, name="nsca%d" % x, align_bytes=64) for x in range(2)]
         acc1 = {}
 
         def MM1(s, x):
-            wc, ws = codes[s + 2], scales[s + 2]
-            acc = accp.tile([P, 512], F32, name="acc1", tag="acc")
+            hc, hs = codes[9 * x], scales[9 * x]
+            wc, ws = codes[s + 1], scales[s + 1]
+            acc = bank("acc1")
             acc1[(s, x)] = acc
             for b2 in range(2):
                 for g in range(4):
@@ -165,7 +181,7 @@ def tile_rnnclassifier_pa_kernel(tc, h1, W_ih1, b_ih1, b_hh1, ln_g, ln_b, fc_W, 
                     rc = slice(g * 256, (g + 1) * 256)
                     nc.tensor.matmul_mx(
                         out=acc[:, b2 * 256:(b2 + 1) * 256],
-                        lhsT=codes[x][:, lc].bitcast(FP8X4), lhsT_scale=scales[x][:, lc],
+                        lhsT=hc[:, lc].bitcast(FP8X4), lhsT_scale=hs[:, lc],
                         rhs=wc[:, rc].bitcast(FP8X4), rhs_scale=ws[:, rc],
                         start=(g == 0), stop=(g == 3),
                     )
@@ -184,14 +200,15 @@ def tile_rnnclassifier_pa_kernel(tc, h1, W_ih1, b_ih1, b_hh1, ln_g, ln_b, fc_W, 
         def BN(bt, g):
             nc.vector.bn_stats(out=stats[:, bt, g, :], in_=h2[:, bt, g * 512:(g + 1) * 512])
 
-        def STATS():
-            for bt in range(4):
+        def STATS(x):
+            for bt in (2 * x, 2 * x + 1):
                 nc.vector.bn_aggr(out=mv[:, bt, :], in_=stats[:, bt, :, :].rearrange("p g s -> p (g s)"))
-            nc.vector.tensor_scalar(out=veps[:], in0=mv[:, :, 1], scalar1=LN_EPS, scalar2=None, op0=ALU.add)
-            nc.gpsimd.tensor_tensor(out=rstd[:], in0=veps[:], in1=mhalf[:], op=ALU.pow)
+            half = slice(2 * x, 2 * x + 2)
+            nc.vector.tensor_scalar(out=veps[:, half], in0=mv[:, half, 1], scalar1=LN_EPS, scalar2=None, op0=ALU.add)
+            nc.gpsimd.tensor_tensor(out=rstd[:, half], in0=veps[:, half], in1=mhalf[:, half], op=ALU.pow)
 
-        def Z(g):
-            for bt in range(4):
+        def Z(x, g):
+            for bt in (2 * x, 2 * x + 1):
                 hv = h2[:, bt, g * 512:(g + 1) * 512]
                 nc.vector.tensor_scalar(out=hv, in0=hv, scalar1=mv[:, bt, 0:1], scalar2=rstd[:, bt:bt + 1],
                                         op0=ALU.subtract, op1=ALU.mult)
@@ -200,160 +217,118 @@ def tile_rnnclassifier_pa_kernel(tc, h1, W_ih1, b_ih1, b_hh1, ln_g, ln_b, fc_W, 
         zts = {}
         gns = {}
 
-        def ZT(g):
-            for h in range(2):
-                planes[(h, g)] = plp.tile([P, 4, 512], BF16, name="planes", tag="planes")
-            for t in range(4):
-                c0 = (2 * g + t // 2) * 256 + (t % 2) * 128
-                zt = tps.tile([P, 512], F32, name="zt", tag="tp")
-                for bt in range(4):
-                    nc.tensor.transpose(zt[:, bt * 128:(bt + 1) * 128], h2[:, bt, c0:c0 + 128], ident[:])
-                zts[(g, t)] = zt
+        def ZT(x, g, u):
+            if u == 0:
+                for h in range(2):
+                    planes[(x, g, h)] = plp.tile([P, 4, 256], BF16, name="planes", tag="planes")
+            zt = bank("zt")
+            for e in range(2):
+                c0 = (2 * g + u) * 256 + e * 128
+                for b2 in range(2):
+                    j = 2 * e + b2
+                    nc.tensor.transpose(zt[:, j * 128:(j + 1) * 128], h2[:, 2 * x + b2, c0:c0 + 128], ident[:])
+            zts[(x, g, u)] = zt
 
-        def GB(g):
+        def GB(x, g, u):
             for h in range(2):
-                for t in range(4):
+                for e in range(2):
+                    t = 2 * u + e
                     col = 16 * h + 4 * g + t
-                    nc.scalar.activation(out=planes[(h, g)][:, t, :], in_=zts[(g, t)][:], func=ACT.Identity,
-                                         scale=gb[:, col:col + 1], bias=gb[:, 32 + col:33 + col])
+                    nc.scalar.activation(out=planes[(x, g, h)][:, t, :], in_=zts[(x, g, u)][:, e * 256:(e + 1) * 256],
+                                         func=ACT.Identity, scale=gb[:, col:col + 1], bias=gb[:, 32 + col:33 + col])
 
-        def RG(g, h):
-            gn = gnp.tile([P, 512, 4], BF16, name="gn", tag="gn", align_bytes=64)
+        def RGQN(x, g, h):
+            gn = gnp.tile([P, 256, 4], BF16, name="gn", tag="gn", align_bytes=64)
             nc.vector.tensor_copy(
                 out=gn[:].rearrange("p (c i) t -> p c t i", i=4),
-                in_=planes[(h, g)][:].rearrange("p t (c i) -> p c t i", i=4),
+                in_=planes[(x, g, h)][:].rearrange("p t (c i) -> p c t i", i=4),
             )
-            gns[(h, g)] = gn
-
-        def QN(g, h):
             kp = 4 * h + g
-            nc.vector.quantize_mx(out=ncod[:, kp * 512:(kp + 1) * 512].bitcast(FP8X4),
-                                  scales=nsca[:, kp * 512:(kp + 1) * 512],
-                                  in_=gns[(h, g)][:].rearrange("p b t -> p (b t)"))
+            nc.vector.quantize_mx(out=ncod[x][:, kp * 256:(kp + 1) * 256].bitcast(FP8X4),
+                                  scales=nsca[x][:, kp * 256:(kp + 1) * 256],
+                                  in_=gn[:].rearrange("p b t -> p (b t)"))
 
         acc2 = {}
 
-        def MM2(cc, kp, bt, first, last):
-            f = 10 + cc * 4 + kp // 2
-            rc = slice((kp % 2) * 512, (kp % 2 + 1) * 512)
-            if first:
-                acc2[bt] = accp.tile([P, 512], F32, name="acc2", tag="acc")
-            lc = slice(kp * 512 + bt * 128, kp * 512 + (bt + 1) * 128)
-            nc.tensor.matmul_mx(
-                out=acc2[bt][:],
-                lhsT=ncod[:, lc].bitcast(FP8X4), lhsT_scale=nsca[:, lc],
-                rhs=codes[f][:, rc].bitcast(FP8X4), rhs_scale=scales[f][:, rc],
-                start=first, stop=last,
-            )
+        def MM2(x, g, h):
+            kp = 4 * h + g
+            f = 10 + 2 * g + h
+            first = g == 0 and h == 0
+            last = g == 3 and h == 1
+            for b2 in range(2):
+                for cc in range(2):
+                    if first:
+                        acc2[(x, b2, cc)] = bank("acc2")
+                    lc = slice(kp * 256 + b2 * 128, kp * 256 + (b2 + 1) * 128)
+                    rc = slice(cc * 512, (cc + 1) * 512)
+                    nc.tensor.matmul_mx(
+                        out=acc2[(x, b2, cc)][:],
+                        lhsT=ncod[x][:, lc].bitcast(FP8X4), lhsT_scale=nsca[x][:, lc],
+                        rhs=codes[f][:, rc].bitcast(FP8X4), rhs_scale=scales[f][:, rc],
+                        start=first, stop=last,
+                    )
+                    if last:
+                        osb = osp.tile([P, 512], F32, name="osb", tag="osb")
+                        nc.vector.tensor_tensor(out=osb[:], in0=acc2[(x, b2, cc)][:], in1=fcb[:, rc], op=ALU.add)
+                        r0 = (2 * x + b2) * 128
+                        nc.sync.dma_start(out=out[r0:r0 + 128, rc], in_=osb[:])
 
-        def MM2all(cc, kp, first, last):
-            for bt in range(4):
-                MM2(cc, kp, bt, first, last)
-
-        def OUT(cc, bt):
-            osb = osp.tile([P, 512], F32, name="osb", tag="osb")
-            nc.vector.tensor_tensor(out=osb[:], in0=acc2[bt][:], in1=fcb[:, cc * 512:(cc + 1) * 512], op=ALU.add)
-            nc.sync.dma_start(out=out[bt * 128:(bt + 1) * 128, cc * 512:(cc + 1) * 512], in_=osb[:])
+        def due(n, start, count):
+            d = n - start
+            if d >= 0 and d % 2 == 0 and d // 2 < count:
+                return d // 2
+            return None
 
         T(0)
-        C(0)
-        load()
+        C(0, 0)
         for c in range(4):
             BM(c)
-        T(2)
-        C(2)
-        load()
+        T(1)
+        C(1, 0)
         Q(0)
         BM(4)
         BM(5)
         GT()
-        T(1)
-        C(1)
-        load()
-        Q(2)
-        MM1(0, 0)
-        T(3)
-        C(3)
-        load()
+        T(2)
+        C(2, 0)
         Q(1)
-        BIAS(0, 0)
-        MM1(0, 1)
-        T(4)
-        T(5)
-        load()
-        load()
-        C(4)
-        Q(3)
-        BIAS(0, 1)
-        for s in range(1, 8):
-            k = s + 2
-            MM1(s, 0)
-            MM1(s, 1)
-            T(k + 3)
-            load()
-            TANH(s - 1, 0)
-            TANH(s - 1, 1)
-            C(k + 2)
-            Q(k + 1)
-            if s % 2 == 0:
-                BN(0, s // 2 - 1)
-                BN(1, s // 2 - 1)
-            elif s > 1:
-                BN(2, s // 2 - 1)
-                BN(3, s // 2 - 1)
-            BIAS(s, 0)
-            BIAS(s, 1)
-        for i in range(4):
-            load()
-        TANH(7, 0)
-        TANH(7, 1)
-        C(12)
-        T(13)
-        C(13)
-        for bt in range(4):
-            BN(bt, 3)
-        STATS()
-        Q(11)
-        Q(12)
-        Z(0)
-        ZT(0)
-        GB(0)
-        Z(1)
-        Q(13)
-        for g in range(4):
-            if g < 3:
-                ZT(g + 1)
-            RG(g, 0)
-            if g < 3:
-                GB(g + 1)
-            RG(g, 1)
-            QN(g, 0)
-            QN(g, 1)
-            if g < 2:
-                Z(g + 2)
-            MM2all(0, g, g == 0, False)
-            MM2all(0, 4 + g, False, g == 3)
-        T(14)
-        C(14, "SSSV")
-        T(15)
-        C(15, "SSSV")
-        Q(14)
-        for bt in range(4):
-            OUT(0, bt)
-        T(16)
-        C(16, "SSSV")
-        Q(15)
-        MM2all(1, 0, True, False)
-        MM2all(1, 1, False, False)
-        T(17)
-        C(17, "SSSV")
-        Q(16)
-        MM2all(1, 2, False, False)
-        MM2all(1, 3, False, False)
-        Q(17)
-        MM2all(1, 4, False, False)
-        MM2all(1, 5, False, False)
-        for bt in range(4):
-            MM2(1, 6, bt, False, False)
-            MM2(1, 7, bt, False, True)
-            OUT(1, bt)
+        T(3)
+        for n in range(N_STEPS):
+            x, s = n // 8, n % 8
+            for xx in range(2):
+                for h in range(2):
+                    g = due(n, N0[xx] + MM_LAG[h], 4)
+                    if g is not None:
+                        MM2(xx, g, h)
+            if n < 16:
+                MM1(s, x)
+            T(n + 4)
+            for xx in range(2):
+                c = n - N0[xx]
+                if 0 <= c < 8:
+                    ZT(xx, c // 2, c % 2)
+            if 1 <= n <= 16:
+                TANH((n - 1) % 8, (n - 1) // 8)
+            C(n + 3, 1 if n >= 10 else 0)
+            for xx in range(2):
+                c = n - N0[xx] - 1
+                if 0 <= c < 8:
+                    GB(xx, c // 2, c % 2)
+            Q(n + 2)
+            if 2 <= n <= 16 and n % 2 == 0:
+                xx, g = (n - 1) // 8, ((n - 1) % 8) // 2
+                BN(2 * xx, g)
+                BN(2 * xx + 1, g)
+                if g == 3:
+                    STATS(xx)
+            for xx in range(2):
+                for h in range(2):
+                    g = due(n, N0[xx] + RG_LAG[h], 4)
+                    if g is not None:
+                        RGQN(xx, g, h)
+            for xx in range(2):
+                g = due(n, N0[xx] - 1, 4)
+                if g is not None:
+                    Z(xx, g)
+            if n < 16:
+                BIAS(s, x)

@@ -135,11 +135,14 @@ def tile_rnnclassifier_pa_kernel(tc, h1, W_ih1, b_ih1, b_hh1, ln_g, ln_b, fc_W, 
         nc.vector.memset(gl[:], 0.0)
         mhalf = const.tile([P, 4], F32, name="mhalf")
         nc.vector.memset(mhalf[:], -0.5)
+        warm = const.tile([P, 1], F32, name="warm")
+        nc.vector.memset(warm[:], 0.0)
         nc.scalar.dma_start(out=brow[0:1, 0:2048], in_=b_ih1.rearrange("(o n) -> o n", o=1))
         nc.scalar.dma_start(out=brow[1:2, 0:2048], in_=b_hh1.rearrange("(o n) -> o n", o=1))
         nc.scalar.dma_start(out=brow[0:1, 2048:3072], in_=fc_b.rearrange("(o n) -> o n", o=1))
         nc.scalar.dma_start(out=gl[0:16, :], in_=ln_g.rearrange("(r c) -> r c", c=256))
         nc.scalar.dma_start(out=gl[16:32, :], in_=ln_b.rearrange("(r c) -> r c", c=256))
+        nc.scalar.activation(out=warm[:], in_=warm[:], func=ACT.Tanh)
 
         bias1 = const.tile([P, 2048], F32, name="bias1")
         fcb = const.tile([P, 1024], F32, name="fcb")
@@ -237,16 +240,19 @@ def tile_rnnclassifier_pa_kernel(tc, h1, W_ih1, b_ih1, b_hh1, ln_g, ln_b, fc_W, 
                     nc.scalar.activation(out=planes[(x, g, h)][:, t, :], in_=zts[(x, g, u)][:, e * 256:(e + 1) * 256],
                                          func=ACT.Identity, scale=gb[:, col:col + 1], bias=gb[:, 32 + col:33 + col])
 
-        def RGQN(x, g, h):
+        def RG(x, g, h):
             gn = gnp.tile([P, 256, 4], BF16, name="gn", tag="gn", align_bytes=64)
             nc.vector.tensor_copy(
                 out=gn[:].rearrange("p (c i) t -> p c t i", i=4),
                 in_=planes[(x, g, h)][:].rearrange("p t (c i) -> p c t i", i=4),
             )
+            gns[(x, g, h)] = gn
+
+        def QN(x, g, h):
             kp = 4 * h + g
             nc.vector.quantize_mx(out=ncod[x][:, kp * 256:(kp + 1) * 256].bitcast(FP8X4),
                                   scales=nsca[x][:, kp * 256:(kp + 1) * 256],
-                                  in_=gn[:].rearrange("p b t -> p (b t)"))
+                                  in_=gns[(x, g, h)][:].rearrange("p b t -> p (b t)"))
 
         acc2 = {}
 
@@ -297,11 +303,16 @@ def tile_rnnclassifier_pa_kernel(tc, h1, W_ih1, b_ih1, b_hh1, ln_g, ln_b, fc_W, 
             x, s = n // 8, n % 8
             for xx in range(2):
                 for h in range(2):
+                    g = due(n, N0[xx] + RG_LAG[h] + 1, 4)
+                    if g is not None:
+                        QN(xx, g, h)
+            if n < 16:
+                MM1(s, x)
+            for xx in range(2):
+                for h in range(2):
                     g = due(n, N0[xx] + MM_LAG[h], 4)
                     if g is not None:
                         MM2(xx, g, h)
-            if n < 16:
-                MM1(s, x)
             T(n + 4)
             for xx in range(2):
                 c = n - N0[xx]
@@ -325,10 +336,10 @@ def tile_rnnclassifier_pa_kernel(tc, h1, W_ih1, b_ih1, b_hh1, ln_g, ln_b, fc_W, 
                 for h in range(2):
                     g = due(n, N0[xx] + RG_LAG[h], 4)
                     if g is not None:
-                        RGQN(xx, g, h)
+                        RG(xx, g, h)
+            if n < 16:
+                BIAS(s, x)
             for xx in range(2):
                 g = due(n, N0[xx] - 1, 4)
                 if g is not None:
                     Z(xx, g)
-            if n < 16:
-                BIAS(s, x)

@@ -34,7 +34,6 @@ def tile_rnnclassifier_pa_kernel(tc, h1, W_ih1, b_ih1, b_hh1, ln_g, ln_b, fc_W, 
         gnp = ctx.enter_context(tc.tile_pool(name="gnorm", bufs=3))
         osp = ctx.enter_context(tc.tile_pool(name="outs", bufs=4))
         psp = ctx.enter_context(tc.psum_pool(name="psum", bufs=8))
-        ctx.enter_context(tc.manual_schedule())
 
         def bank(name):
             return psp.tile([P, 512], F32, name=name, tag="ps")

from contextlib import ExitStack

import concourse.mybir as mybir
from concourse.masks import make_identity

F32 = mybir.dt.float32
BF16 = mybir.dt.bfloat16
U32 = mybir.dt.uint32
U8 = mybir.dt.uint8
FP8X4 = mybir.dt.float8_e4m3fn_x4
ALU = mybir.AluOpType
ACT = mybir.ActivationFunctionType

P = 128
B, H, D_OUT = 512, 2048, 1024
LN_EPS = 1e-5
FLOPS = 2 * B * H * H + 2 * B * 2 * H * D_OUT


N0 = (10, 17)
RG_LAG = (3, 4)
MM_LAG = (4, 5)
N_STEPS = 29


def tile_rnnclassifier_pa_kernel(tc, h1, W_ih1, b_ih1, b_hh1, ln_g, ln_b, fc_W, fc_b, out):
    nc = tc.nc
    with ExitStack() as ctx:
        const = ctx.enter_context(tc.tile_pool(name="const", bufs=1))
        rawp = ctx.enter_context(tc.tile_pool(name="raw", bufs=4))
        grpp = ctx.enter_context(tc.tile_pool(name="grouped", bufs=3))
        wfp = ctx.enter_context(tc.tile_pool(name="wfcodes", bufs=10))
        plp = ctx.enter_context(tc.tile_pool(name="planes", bufs=4))
        gnp = ctx.enter_context(tc.tile_pool(name="gnorm", bufs=3))
        osp = ctx.enter_context(tc.tile_pool(name="outs", bufs=4))
        psp = ctx.enter_context(tc.psum_pool(name="psum", bufs=8))

        def bank(name):
            return psp.tile([P, 512], F32, name=name, tag="ps")

        def slab_off(pos, i, a, u):
            if pos == 0 or pos == 9:
                return (i // 2) * 1024 + (2 * (i % 2) + a) * 256 + u * 128
            if pos < 9:
                return a * 1024 + i * 256 + u * 128
            return (2 * i + a) * 256 + u * 128

        raws = {}
        banks = {}
        groupeds = {}
        codes = {}
        scales = {}
        loaded = []

        def load():
            pos = len(loaded)
            if pos >= 18:
                return
            loaded.append(pos)
            raw = rawp.tile([P, 4096], BF16, name="raw", tag="raw")
            raws[pos] = raw
            if pos == 0:
                for i in range(4):
                    nc.sync.dma_start(
                        out=raw[:, i * 1024:(i + 1) * 1024],
                        in_=h1[(i // 2) * 128:(i // 2 + 1) * 128, (i % 2) * 1024:(i % 2 + 1) * 1024],
                    )
            elif pos == 9:
                nc.sync.dma_start(out=raw[:].rearrange("p (t k) -> p t k", t=2),
                                  in_=h1[256:512, :].rearrange("(t p) k -> p t k", p=P))
            elif pos < 9:
                s = pos - 1
                nc.sync.dma_start(out=raw[:], in_=W_ih1[s * 256:(s + 1) * 256, :].rearrange("(q e) k -> q (e k)", e=2))
            else:
                f = pos - 10
                kp = 4 * (f % 2) + f // 2
                nc.sync.dma_start(
                    out=raw[:].rearrange("p (c k) -> p c k", c=8),
                    in_=fc_W[:, kp * 512:(kp + 1) * 512].rearrange("(c p) k -> p c k", p=P),
                )

        def T(pos):
            if pos >= 18:
                return
            raw_w = raws[pos][:].bitcast(F32)
            banks[pos] = []
            for i in range(4):
                xt = bank("xt")
                for a in range(2):
                    for u in range(2):
                        o = slab_off(pos, i, a, u)
                        j = 2 * a + u
                        nc.tensor.transpose(xt[:, j * 128:(j + 1) * 128], raw_w[:, o:o + 128], ident[:])
                banks[pos].append(xt)
            load()

        def C(pos, vector_share):
            if pos >= 18:
                return
            grouped = grpp.tile([P, 4096], BF16, name="grouped", tag="grouped", align_bytes=64)
            gw = grouped[:].bitcast(F32)
            for i in range(4):
                dst = gw[:, i * 512:(i + 1) * 512].rearrange("p (a c u) -> p a c u", a=2, u=2)
                src = banks[pos][i][:].rearrange("p (a u c) -> p a c u", a=2, u=2)
                if i >= 4 - vector_share:
                    nc.vector.tensor_copy(out=dst, in_=src)
                else:
                    nc.scalar.copy(out=dst, in_=src)
            groupeds[pos] = grouped

        def Q(pos):
            if pos >= 18:
                return
            if pos == 0 or pos == 9:
                cd = const.tile([P, 1024], U32, name="hcd%d" % pos, align_bytes=64)
                sc = const.tile([P, 1024], U8, name="hsc%d" % pos, align_bytes=64)
            else:
                cd = wfp.tile([P, 1024], U32, name="cd", tag="cd", align_bytes=64)
                sc = wfp.tile([P, 1024], U8, name="sc", tag="sc", align_bytes=64)
            nc.vector.quantize_mx(out=cd[:].bitcast(FP8X4), scales=sc[:], in_=groupeds[pos][:])
            codes[pos] = cd
            scales[pos] = sc

        for i in range(4):
            load()

        ident = const.tile([P, P], F32, name="ident")
        make_identity(nc, ident[:])
        ones = const.tile([P, P], BF16, name="ones")
        nc.vector.memset(ones[:], 1.0)
        brow = const.tile([P, 3072], BF16, name="brow")
        nc.vector.memset(brow[:], 0.0)
        gl = const.tile([P, 256], BF16, name="gl")
        nc.vector.memset(gl[:], 0.0)
        mhalf = const.tile([P, 4], F32, name="mhalf")
        nc.vector.memset(mhalf[:], -0.5)
        warm = const.tile([P, 1], F32, name="warm")
        nc.vector.memset(warm[:], 0.0)
        nc.scalar.dma_start(out=brow[0:1, 0:2048], in_=b_ih1.rearrange("(o n) -> o n", o=1))
        nc.scalar.dma_start(out=brow[1:2, 0:2048], in_=b_hh1.rearrange("(o n) -> o n", o=1))
        nc.scalar.dma_start(out=brow[0:1, 2048:3072], in_=fc_b.rearrange("(o n) -> o n", o=1))
        nc.scalar.dma_start(out=gl[0:16, :], in_=ln_g.rearrange("(r c) -> r c", c=256))
        nc.scalar.dma_start(out=gl[16:32, :], in_=ln_b.rearrange("(r c) -> r c", c=256))
        nc.scalar.activation(out=warm[:], in_=warm[:], func=ACT.Tanh)

        bias1 = const.tile([P, 2048], F32, name="bias1")
        fcb = const.tile([P, 1024], F32, name="fcb")
        gb = const.tile([P, 64], F32, name="gb")

        def BM(c):
            bp = bank("bp")
            nc.tensor.matmul(out=bp[:], lhsT=ones[:], rhs=brow[:, c * 512:(c + 1) * 512], start=True, stop=True)
            if c < 4:
                nc.vector.tensor_copy(
                    out=bias1[:, c * 512:(c + 1) * 512].rearrange("p (s e q) -> p s e q", s=2, e=2),
                    in_=bp[:].rearrange("p (s q e) -> p s e q", s=2, e=2),
                )
            else:
                nc.vector.tensor_copy(out=fcb[:, (c - 4) * 512:(c - 3) * 512], in_=bp[:])

        def GT():
            gps = bank("gps")
            nc.tensor.transpose(gps[:, 0:128], gl[:].bitcast(F32), ident[:])
            nc.vector.tensor_copy(out=gb[:], in_=gps[:, 0:32].bitcast(BF16))

        h2 = const.tile([P, 4, 2048], F32, name="h2")
        stats = const.tile([P, 4, 4, 6], F32, name="stats")
        mv = const.tile([P, 4, 2], F32, name="mv")
        veps = const.tile([P, 4], F32, name="veps")
        rstd = const.tile([P, 4], F32, name="rstd")
        ncod = [const.tile([P, 8 * 256], U32, name="ncod%d" % x, align_bytes=64) for x in range(2)]
        nsca = [const.tile([P, 8 * 256], U8, name="nsca%d" % x, align_bytes=64) for x in range(2)]
        acc1 = {}

        def MM1(s, x):
            hc, hs = codes[9 * x], scales[9 * x]
            wc, ws = codes[s + 1], scales[s + 1]
            acc = bank("acc1")
            acc1[(s, x)] = acc
            for b2 in range(2):
                for g in range(4):
                    lc = slice((b2 * 4 + g) * 128, (b2 * 4 + g + 1) * 128)
                    rc = slice(g * 256, (g + 1) * 256)
                    nc.tensor.matmul_mx(
                        out=acc[:, b2 * 256:(b2 + 1) * 256],
                        lhsT=hc[:, lc].bitcast(FP8X4), lhsT_scale=hs[:, lc],
                        rhs=wc[:, rc].bitcast(FP8X4), rhs_scale=ws[:, rc],
                        start=(g == 0), stop=(g == 3),
                    )

        def BIAS(s, x):
            nc.vector.tensor_tensor(
                out=h2[:, 2 * x:2 * x + 2, s * 256:(s + 1) * 256],
                in0=acc1[(s, x)][:].rearrange("p (b n) -> p b n", b=2),
                in1=bias1[:, s * 256:(s + 1) * 256].unsqueeze(1).to_broadcast([P, 2, 256]), op=ALU.add,
            )

        def TANH(s, x):
            hv = h2[:, 2 * x:2 * x + 2, s * 256:(s + 1) * 256]
            nc.scalar.activation(out=hv, in_=hv, func=ACT.Tanh)

        def BN(bt, g):
            nc.vector.bn_stats(out=stats[:, bt, g, :], in_=h2[:, bt, g * 512:(g + 1) * 512])

        def STATS(x):
            for bt in (2 * x, 2 * x + 1):
                nc.vector.bn_aggr(out=mv[:, bt, :], in_=stats[:, bt, :, :].rearrange("p g s -> p (g s)"))
            half = slice(2 * x, 2 * x + 2)
            nc.vector.tensor_scalar(out=veps[:, half], in0=mv[:, half, 1], scalar1=LN_EPS, scalar2=None, op0=ALU.add)
            nc.gpsimd.tensor_tensor(out=rstd[:, half], in0=veps[:, half], in1=mhalf[:, half], op=ALU.pow)

        def Z(x, g):
            for bt in (2 * x, 2 * x + 1):
                hv = h2[:, bt, g * 512:(g + 1) * 512]
                nc.vector.tensor_scalar(out=hv, in0=hv, scalar1=mv[:, bt, 0:1], scalar2=rstd[:, bt:bt + 1],
                                        op0=ALU.subtract, op1=ALU.mult)

        planes = {}
        zts = {}
        gns = {}

        def ZT(x, g, u):
            if u == 0:
                for h in range(2):
                    planes[(x, g, h)] = plp.tile([P, 4, 256], BF16, name="planes", tag="planes")
            zt = bank("zt")
            for e in range(2):
                c0 = (2 * g + u) * 256 + e * 128
                for b2 in range(2):
                    j = 2 * e + b2
                    nc.tensor.transpose(zt[:, j * 128:(j + 1) * 128], h2[:, 2 * x + b2, c0:c0 + 128], ident[:])
            zts[(x, g, u)] = zt

        def GB(x, g, u):
            for h in range(2):
                for e in range(2):
                    t = 2 * u + e
                    col = 16 * h + 4 * g + t
                    nc.scalar.activation(out=planes[(x, g, h)][:, t, :], in_=zts[(x, g, u)][:, e * 256:(e + 1) * 256],
                                         func=ACT.Identity, scale=gb[:, col:col + 1], bias=gb[:, 32 + col:33 + col])

        def RG(x, g, h):
            gn = gnp.tile([P, 256, 4], BF16, name="gn", tag="gn", align_bytes=64)
            nc.vector.tensor_copy(
                out=gn[:].rearrange("p (c i) t -> p c t i", i=4),
                in_=planes[(x, g, h)][:].rearrange("p t (c i) -> p c t i", i=4),
            )
            gns[(x, g, h)] = gn

        def QN(x, g, h):
            kp = 4 * h + g
            nc.vector.quantize_mx(out=ncod[x][:, kp * 256:(kp + 1) * 256].bitcast(FP8X4),
                                  scales=nsca[x][:, kp * 256:(kp + 1) * 256],
                                  in_=gns[(x, g, h)][:].rearrange("p b t -> p (b t)"))

        acc2 = {}

        def MM2(x, g, h):
            kp = 4 * h + g
            f = 10 + 2 * g + h
            first = g == 0 and h == 0
            last = g == 3 and h == 1
            for b2 in range(2):
                for cc in range(2):
                    if first:
                        acc2[(x, b2, cc)] = bank("acc2")
                    lc = slice(kp * 256 + b2 * 128, kp * 256 + (b2 + 1) * 128)
                    rc = slice(cc * 512, (cc + 1) * 512)
                    nc.tensor.matmul_mx(
                        out=acc2[(x, b2, cc)][:],
                        lhsT=ncod[x][:, lc].bitcast(FP8X4), lhsT_scale=nsca[x][:, lc],
                        rhs=codes[f][:, rc].bitcast(FP8X4), rhs_scale=scales[f][:, rc],
                        start=first, stop=last,
                    )
                    if last:
                        osb = osp.tile([P, 512], F32, name="osb", tag="osb")
                        nc.vector.tensor_tensor(out=osb[:], in0=acc2[(x, b2, cc)][:], in1=fcb[:, rc], op=ALU.add)
                        r0 = (2 * x + b2) * 128
                        nc.sync.dma_start(out=out[r0:r0 + 128, rc], in_=osb[:])

        def due(n, start, count):
            d = n - start
            if d >= 0 and d % 2 == 0 and d // 2 < count:
                return d // 2
            return None

        T(0)
        C(0, 0)
        for c in range(4):
            BM(c)
        T(1)
        C(1, 0)
        Q(0)
        BM(4)
        BM(5)
        GT()
        T(2)
        C(2, 0)
        Q(1)
        T(3)
        for n in range(N_STEPS):
            x, s = n // 8, n % 8
            for xx in range(2):
                for h in range(2):
                    g = due(n, N0[xx] + RG_LAG[h] + 1, 4)
                    if g is not None:
                        QN(xx, g, h)
            if n < 16:
                MM1(s, x)
            for xx in range(2):
                for h in range(2):
                    g = due(n, N0[xx] + MM_LAG[h], 4)
                    if g is not None:
                        MM2(xx, g, h)
            T(n + 4)
            for xx in range(2):
                c = n - N0[xx]
                if 0 <= c < 8:
                    ZT(xx, c // 2, c % 2)
            if 1 <= n <= 16:
                TANH((n - 1) % 8, (n - 1) // 8)
            C(n + 3, 1 if n >= 10 else 0)
            for xx in range(2):
                c = n - N0[xx] - 1
                if 0 <= c < 8:
                    GB(xx, c // 2, c % 2)
            Q(n + 2)
            if 2 <= n <= 16 and n % 2 == 0:
                xx, g = (n - 1) // 8, ((n - 1) % 8) // 2
                BN(2 * xx, g)
                BN(2 * xx + 1, g)
                if g == 3:
                    STATS(xx)
            for xx in range(2):
                for h in range(2):
                    g = due(n, N0[xx] + RG_LAG[h], 4)
                    if g is not None:
                        RG(xx, g, h)
            if n < 16:
                BIAS(s, x)
            for xx in range(2):
                g = due(n, N0[xx] - 1, 4)
                if g is not None:
                    Z(xx, g)
